import numpy as np
import ml_dtypes


def mxq(x, axis, fmt="e4m3"):
    dtype, down = {"e4m3": (ml_dtypes.float8_e4m3fn, 7), "e5m2": (ml_dtypes.float8_e5m2, 14)}[fmt]
    v = np.moveaxis(np.asarray(x, np.float32).astype(ml_dtypes.bfloat16).astype(np.float64), axis, -1)
    blocks = v.reshape(v.shape[:-1] + (-1, 32))
    amax = np.abs(blocks).max(-1, keepdims=True)
    byte = np.maximum(np.where(amax > 0, np.frexp(amax)[1] - 1 + 127, 0) - down, 1)
    scale = np.exp2(byte - 127.0)
    codes = (blocks / scale).astype(np.float32).astype(dtype).astype(np.float64)
    return np.moveaxis((codes * scale).reshape(v.shape), -1, axis)


WIDE = False


def mx_kscale(k):
    if not WIDE:
        return np.ones(k)
    levels = np.array([10, -10, 5, -5, 0])
    a = np.random.permutation(np.resize(levels, k // 512 * 4)).reshape(k // 512, 4)
    idx = np.arange(k)
    return np.exp2(a[idx // 512, idx % 128 // 32])


BF16 = ml_dtypes.bfloat16


def bf(x):
    return np.asarray(x, np.float32).astype(BF16)


def f64(x):
    return np.asarray(x).astype(np.float64)


B, N, C, DIN, H, KS, KC = 1, 1024, 4, 64, 64, 3, 3


def setup_inputs():
    s = mx_kscale(N)
    sn = s[None, :, None, None]
    return {"Gs": bf(np.random.standard_normal((N, N)) * 0.5 / np.sqrt(N) * s[None, :] / s[:, None]),
            "Xt": bf(np.random.standard_normal((B, N, C, DIN)) * sn),
            "Ht_1": bf(np.random.standard_normal((B, N, C, H)) * sn)}


def reference(Gs, Xt, Ht_1):
    g = f64(Gs)
    g0 = mxq(g, 0, "e4m3")
    t2 = 2.0 * (mxq(g, 1, "e4m3") @ g0) - np.eye(N)
    xh = np.concatenate([f64(Xt), f64(Ht_1)], axis=-1)
    xq = mxq(xh.transpose(0, 2, 3, 1), 3, "e4m3")
    x1 = (xq @ g0).transpose(0, 3, 1, 2)
    x2 = (xq @ mxq(t2, 0, "e4m3")).transpose(0, 3, 1, 2)
    return x1, x2

@@ -1,0 +1,223 @@
+from contextlib import ExitStack
+
+import concourse.mybir as mybir
+from concourse.masks import make_identity
+
+BF16 = mybir.dt.bfloat16
+F32 = mybir.dt.float32
+U32 = mybir.dt.uint32
+U8 = mybir.dt.uint8
+FP8X4 = mybir.dt.float8_e4m3fn_x4
+COPY = mybir.ActivationFunctionType.Copy
+MULT = mybir.AluOpType.mult
+SUBTRACT = mybir.AluOpType.subtract
+
+P = 128
+PACK = 4
+K_PASS = P * PACK
+NODES = 1024
+PASSES = NODES // K_PASS
+TILES = NODES // P
+CHANNELS = 4
+HALF_FEATS = 64
+SOURCE_FEATS = CHANNELS * HALF_FEATS
+FEATS = 2 * SOURCE_FEATS
+QUARTER = NODES // 4
+HALF = NODES // 2
+
+FLOPS = 2 * NODES * NODES * NODES + 2 * 2 * NODES * NODES * FEATS
+
+
+def quantise(nc, grouped, codes, scales):
+    nc.vector.quantize_mx(out=codes.bitcast(FP8X4), scales=scales, in_=grouped)
+
+
+def regroup(copy, grouped, rows):
+    copy(
+        out=grouped.rearrange("p (c i) t -> p c t i", i=4),
+        in_=rows.rearrange("p t (c i) -> p c t i", i=4),
+    )
+
+
+def tile_stc_cell_pa_kernel(tc, Gs, Xt, Ht_1, out_0, out_1):
+    nc = tc.nc
+    with ExitStack() as stack:
+        keep = stack.enter_context(tc.tile_pool(name="keep", bufs=1))
+        psum = stack.enter_context(tc.psum_pool(name="psum", bufs=8))
+        stack.enter_context(tc.manual_schedule())
+
+        g_rows = keep.tile([P, PASSES * PACK, NODES], BF16)
+        g_dram = Gs.rearrange("(g p t) m -> g p t m", g=PASSES, t=PACK)
+        for g in range(PASSES):
+            for pair in range(2):
+                nc.sync.dma_start(
+                    out=g_rows[:, PACK * g + 2 * pair : PACK * g + 2 * pair + 2, :],
+                    in_=g_dram[g][:, 2 * pair : 2 * pair + 2, :],
+                )
+        x_rows = keep.tile([P, 2, PASSES, PACK, SOURCE_FEATS], BF16)
+        for s, source in enumerate((Xt, Ht_1)):
+            nc.sync.dma_start(
+                out=x_rows[:, s, :, :, :].rearrange("p g t f -> p g (t f)"),
+                in_=source.rearrange("b (g p t) c l -> p (b g) (t c l)", g=PASSES, t=PACK),
+            )
+
+        ident = keep.tile([P, P], F32)
+        make_identity(nc, ident[:])
+        eye = keep.tile([P, K_PASS, PACK], BF16)
+        nc.vector.memset(eye[:], 0.0)
+        nc.vector.tensor_copy(
+            out=eye[:].rearrange("p (q a) t -> p q (a t)", a=PACK)[:, :, 0 : PACK * PACK : PACK + 1],
+            in_=ident[:].unsqueeze(2).to_broadcast([P, P, PACK]),
+        )
+
+        left_grouped = keep.tile([P, PASSES, NODES * PACK], BF16, align_bytes=64)
+        left_codes = keep.tile([P, PASSES, NODES], U32, align_bytes=64)
+        left_scales = keep.tile([P, PASSES, NODES], U8, align_bytes=64)
+        g_grouped = keep.tile([P, PASSES, NODES, PACK], BF16, align_bytes=64)
+        g_codes = keep.tile([P, PASSES, NODES], U32, align_bytes=64)
+        g_scales = keep.tile([P, PASSES, NODES], U8, align_bytes=64)
+        t2_grouped = keep.tile([P, PASSES, NODES, PACK], BF16, align_bytes=64)
+        t2_codes = keep.tile([P, PASSES, NODES], U32, align_bytes=64)
+        t2_scales = keep.tile([P, PASSES, NODES], U8, align_bytes=64)
+        x_grouped = keep.tile([P, PASSES, FEATS, PACK], BF16, align_bytes=64)
+        x_codes = keep.tile([P, PASSES, FEATS], U32, align_bytes=64)
+        x_scales = keep.tile([P, PASSES, FEATS], U8, align_bytes=64)
+        x1_sb = keep.tile([P, TILES, FEATS], F32)
+        x2_sb = keep.tile([P, TILES, FEATS], F32)
+
+        def flip_rows(g):
+            for pair in range(2):
+                for h in range(PASSES):
+                    flipped = psum.tile([P, 2, 2, P], F32, tag="bank")
+                    for i in range(2):
+                        words = (
+                            g_rows[:, PACK * g + 2 * pair + i, :]
+                            .bitcast(F32)
+                            .rearrange("p (h q u) -> p h u q", h=PASSES, u=2)
+                        )
+                        for u in range(2):
+                            nc.tensor.transpose(flipped[:, i, u, :], words[:, h, u, :], ident[:])
+                    first = (PACK * g + 2 * pair) * P * PACK
+                    nc.scalar.copy(
+                        out=left_grouped[:, h, first : first + 2 * P * PACK]
+                        .bitcast(F32)
+                        .rearrange("q (i p u) -> q i p u", i=2, u=2),
+                        in_=flipped[:].rearrange("q i u p -> q i p u"),
+                    )
+
+        def quantise_left(g):
+            for h in range(PASSES):
+                quantise(
+                    nc,
+                    left_grouped[:, h, HALF * PACK * g : HALF * PACK * (g + 1)],
+                    left_codes[:, h, HALF * g : HALF * (g + 1)],
+                    left_scales[:, h, HALF * g : HALF * (g + 1)],
+                )
+
+        def regroup_g(copy, h, first, width):
+            cols = slice(first, first + width)
+            regroup(copy, g_grouped[:, h, cols, :], g_rows[:, PACK * h : PACK * (h + 1), cols])
+
+        def quantise_g(h, half):
+            cols = slice(HALF * half, HALF * (half + 1))
+            quantise(
+                nc,
+                g_grouped[:, h, cols, :].rearrange("p m t -> p (m t)"),
+                g_codes[:, h, cols],
+                g_scales[:, h, cols],
+            )
+
+        flip_rows(0)
+        regroup_g(nc.vector.tensor_copy, 0, 0, HALF)
+        regroup_g(nc.vector.tensor_copy, 0, HALF, QUARTER)
+        regroup_g(nc.scalar.copy, 0, HALF + QUARTER, QUARTER)
+        quantise_g(0, 0)
+        quantise_left(0)
+        flip_rows(1)
+        regroup_g(nc.vector.tensor_copy, 1, 0, HALF)
+        regroup_g(nc.vector.tensor_copy, 1, HALF, QUARTER)
+        regroup_g(nc.scalar.copy, 1, HALF + QUARTER, QUARTER)
+        quantise_g(1, 0)
+        quantise_g(0, 1)
+        quantise_g(1, 1)
+        quantise_left(1)
+
+        for g in range(PASSES):
+            for s in range(2):
+                regroup(
+                    nc.scalar.copy,
+                    x_grouped[:, g, SOURCE_FEATS * s : SOURCE_FEATS * (s + 1), :],
+                    x_rows[:, s, g, :, :],
+                )
+
+        for g in range(PASSES):
+            for w in range(TILES):
+                cols = slice(P * w, P * (w + 1))
+                product = psum.tile([P, PACK, P], F32, tag="bank")
+                for t in range(PACK):
+                    rows = slice(P * (PACK * g + t), P * (PACK * g + t + 1))
+                    for h in range(PASSES):
+                        nc.tensor.matmul_mx(
+                            out=product[:, t, :],
+                            lhsT=left_codes[:, h, rows].bitcast(FP8X4),
+                            lhsT_scale=left_scales[:, h, rows],
+                            rhs=g_codes[:, h, cols].bitcast(FP8X4),
+                            rhs_scale=g_scales[:, h, cols],
+                            start=(h == 0),
+                            stop=(h == PASSES - 1),
+                        )
+                if w // PACK == g:
+                    nc.vector.scalar_tensor_tensor(
+                        out=t2_grouped[:, g, cols, :],
+                        in0=product[:].rearrange("p t m -> p m t"),
+                        scalar=2.0,
+                        in1=eye[:, P * (w % PACK) : P * (w % PACK + 1), :],
+                        op0=MULT,
+                        op1=SUBTRACT,
+                    )
+                else:
+                    nc.scalar.activation(
+                        out=t2_grouped[:, g, cols, :],
+                        in_=product[:].rearrange("p t m -> p m t"),
+                        func=COPY,
+                        scale=2.0,
+                    )
+            if g == 0:
+                for k in range(PASSES):
+                    quantise(
+                        nc,
+                        x_grouped[:, k, :, :].rearrange("p f t -> p (f t)"),
+                        x_codes[:, k, :],
+                        x_scales[:, k, :],
+                    )
+            quantise(
+                nc,
+                t2_grouped[:, g, :, :].rearrange("p m t -> p (m t)"),
+                t2_codes[:, g, :],
+                t2_scales[:, g, :],
+            )
+
+        for codes, scales, result, out in (
+            (g_codes, g_scales, x1_sb, out_0),
+            (t2_codes, t2_scales, x2_sb, out_1),
+        ):
+            out_view = out.rearrange("b (m p) c l -> p (b m) (c l)", p=P)
+            for m in range(TILES):
+                cols = slice(P * m, P * (m + 1))
+                acc = psum.tile([P, FEATS], F32, tag="bank")
+                for g in range(PASSES):
+                    nc.tensor.matmul_mx(
+                        out=acc[:],
+                        lhsT=codes[:, g, cols].bitcast(FP8X4),
+                        lhsT_scale=scales[:, g, cols],
+                        rhs=x_codes[:, g, :].bitcast(FP8X4),
+                        rhs_scale=x_scales[:, g, :],
+                        start=(g == 0),
+                        stop=(g == PASSES - 1),
+                    )
+                copy = nc.scalar.copy if m % 2 == 0 else nc.vector.tensor_copy
+                copy(
+                    out=result[:, m, :].rearrange("p (c s l) -> p s c l", c=CHANNELS, s=2),
+                    in_=acc[:].rearrange("p (s c l) -> p s c l", s=2, c=CHANNELS),
+                )
+                nc.sync.dma_start(out=out_view[:, m, :], in_=result[:, m, :])

@@ -114,41 +114,41 @@ def tile_stc_cell_pa_kernel(tc, Gs, Xt, Ht_1, out_0, out_1):
                     left_scales[:, h, HALF * g : HALF * (g + 1)],
                 )
 
-        def regroup_g(copy, h, first, width):
-            cols = slice(first, first + width)
-            regroup(copy, g_grouped[:, h, cols, :], g_rows[:, PACK * h : PACK * (h + 1), cols])
+        def prepare_g(passes, quarters):
+            for h in passes:
+                for quarter in quarters:
+                    cols = slice(QUARTER * quarter, QUARTER * (quarter + 1))
+                    regroup(
+                        nc.scalar.copy if quarter == 3 else nc.vector.tensor_copy,
+                        g_grouped[:, h, cols, :],
+                        g_rows[:, PACK * h : PACK * (h + 1), cols],
+                    )
+            for h in passes:
+                for quarter in quarters:
+                    cols = slice(QUARTER * quarter, QUARTER * (quarter + 1))
+                    quantise(
+                        nc,
+                        g_grouped[:, h, cols, :].rearrange("p m t -> p (m t)"),
+                        g_codes[:, h, cols],
+                        g_scales[:, h, cols],
+                    )
 
-        def quantise_g(h, half):
-            cols = slice(HALF * half, HALF * (half + 1))
-            quantise(
-                nc,
-                g_grouped[:, h, cols, :].rearrange("p m t -> p (m t)"),
-                g_codes[:, h, cols],
-                g_scales[:, h, cols],
-            )
-
-        flip_rows(0)
-        regroup_g(nc.vector.tensor_copy, 0, 0, HALF)
-        regroup_g(nc.vector.tensor_copy, 0, HALF, QUARTER)
-        regroup_g(nc.scalar.copy, 0, HALF + QUARTER, QUARTER)
-        quantise_g(0, 0)
-        quantise_left(0)
-        flip_rows(1)
-        regroup_g(nc.vector.tensor_copy, 1, 0, HALF)
-        regroup_g(nc.vector.tensor_copy, 1, HALF, QUARTER)
-        regroup_g(nc.scalar.copy, 1, HALF + QUARTER, QUARTER)
-        quantise_g(1, 0)
-        quantise_g(0, 1)
-        quantise_g(1, 1)
-        quantise_left(1)
-
-        for g in range(PASSES):
-            for s in range(2):
+        def regroup_x(copy, s):
+            for g in range(PASSES):
                 regroup(
-                    nc.scalar.copy,
+                    copy,
                     x_grouped[:, g, SOURCE_FEATS * s : SOURCE_FEATS * (s + 1), :],
                     x_rows[:, s, g, :, :],
                 )
+
+        flip_rows(0)
+        prepare_g((0,), (0, 1))
+        quantise_left(0)
+        flip_rows(1)
+        prepare_g((1,), (0, 1))
+        prepare_g((0, 1), (2, 3))
+        quantise_left(1)
+        regroup_x(nc.scalar.copy, 0)
 
         for g in range(PASSES):
             for w in range(TILES):
@@ -183,6 +183,7 @@ def tile_stc_cell_pa_kernel(tc, Gs, Xt, Ht_1, out_0, out_1):
                         scale=2.0,
                     )
             if g == 0:
+                regroup_x(nc.vector.tensor_copy, 1)
                 for k in range(PASSES):
                     quantise(
                         nc,
@@ -215,7 +216,7 @@ def tile_stc_cell_pa_kernel(tc, Gs, Xt, Ht_1, out_0, out_1):
                         start=(g == 0),
                         stop=(g == PASSES - 1),
                     )
-                copy = nc.scalar.copy if m % 2 == 0 else nc.vector.tensor_copy
+                copy = nc.vector.tensor_copy if (out is out_1 and m % 2 == 1) else nc.scalar.copy
                 copy(
                     out=result[:, m, :].rearrange("p (c s l) -> p s c l", c=CHANNELS, s=2),
                     in_=acc[:].rearrange("p (s c l) -> p s c l", s=2, c=CHANNELS),

@@ -24,6 +24,7 @@ SOURCE_FEATS = CHANNELS * HALF_FEATS
 FEATS = 2 * SOURCE_FEATS
 QUARTER = NODES // 4
 HALF = NODES // 2
+WINDOWS_AFTER_X1 = 2
 
 FLOPS = 2 * NODES * NODES * NODES + 2 * 2 * NODES * NODES * FEATS
 
@@ -150,8 +151,8 @@ def tile_stc_cell_pa_kernel(tc, Gs, Xt, Ht_1, out_0, out_1):
         quantise_left(1)
         regroup_x(nc.scalar.copy, 0)
 
-        for g in range(PASSES):
-            for w in range(TILES):
+        def product_windows(g, windows):
+            for w in windows:
                 cols = slice(P * w, P * (w + 1))
                 product = psum.tile([P, PACK, P], F32, tag="bank")
                 for t in range(PACK):
@@ -182,26 +183,17 @@ def tile_stc_cell_pa_kernel(tc, Gs, Xt, Ht_1, out_0, out_1):
                         func=COPY,
                         scale=2.0,
                     )
-            if g == 0:
-                regroup_x(nc.vector.tensor_copy, 1)
-                for k in range(PASSES):
-                    quantise(
-                        nc,
-                        x_grouped[:, k, :, :].rearrange("p f t -> p (f t)"),
-                        x_codes[:, k, :],
-                        x_scales[:, k, :],
-                    )
+
+        def quantise_t2(g, half):
+            cols = slice(HALF * half, HALF * (half + 1))
             quantise(
                 nc,
-                t2_grouped[:, g, :, :].rearrange("p m t -> p (m t)"),
-                t2_codes[:, g, :],
-                t2_scales[:, g, :],
+                t2_grouped[:, g, cols, :].rearrange("p m t -> p (m t)"),
+                t2_codes[:, g, cols],
+                t2_scales[:, g, cols],
             )
 
-        for codes, scales, result, out in (
-            (g_codes, g_scales, x1_sb, out_0),
-            (t2_codes, t2_scales, x2_sb, out_1),
-        ):
+        def diffuse(codes, scales, result, out, odd_copy):
             out_view = out.rearrange("b (m p) c l -> p (b m) (c l)", p=P)
             for m in range(TILES):
                 cols = slice(P * m, P * (m + 1))
@@ -216,9 +208,28 @@ def tile_stc_cell_pa_kernel(tc, Gs, Xt, Ht_1, out_0, out_1):
                         start=(g == 0),
                         stop=(g == PASSES - 1),
                     )
-                copy = nc.vector.tensor_copy if (out is out_1 and m % 2 == 1) else nc.scalar.copy
+                copy = odd_copy if m % 2 == 1 else nc.scalar.copy
                 copy(
                     out=result[:, m, :].rearrange("p (c s l) -> p s c l", c=CHANNELS, s=2),
                     in_=acc[:].rearrange("p (s c l) -> p s c l", s=2, c=CHANNELS),
                 )
                 nc.sync.dma_start(out=out_view[:, m, :], in_=result[:, m, :])
+
+        product_windows(0, range(TILES))
+        regroup_x(nc.vector.tensor_copy, 1)
+        for g in range(PASSES):
+            quantise(
+                nc,
+                x_grouped[:, g, :, :].rearrange("p f t -> p (f t)"),
+                x_codes[:, g, :],
+                x_scales[:, g, :],
+            )
+        quantise_t2(0, 0)
+        quantise_t2(0, 1)
+        product_windows(1, range(TILES // 2))
+        quantise_t2(1, 0)
+        product_windows(1, range(TILES // 2, TILES - WINDOWS_AFTER_X1))
+        diffuse(g_codes, g_scales, x1_sb, out_0, nc.scalar.copy)
+        product_windows(1, range(TILES - WINDOWS_AFTER_X1, TILES))
+        quantise_t2(1, 1)
+        diffuse(t2_codes, t2_scales, x2_sb, out_1, nc.vector.tensor_copy)

@@ -23,21 +23,8 @@ HALF_FEATS = 64
 SOURCE_FEATS = CHANNELS * HALF_FEATS
 FEATS = 2 * SOURCE_FEATS
 QUARTER = NODES // 4
-HALF = NODES // 2
-WINDOWS_AFTER_X1 = 2
 
 FLOPS = 2 * NODES * NODES * NODES + 2 * 2 * NODES * NODES * FEATS
-
-
-def quantise(nc, grouped, codes, scales):
-    nc.vector.quantize_mx(out=codes.bitcast(FP8X4), scales=scales, in_=grouped)
-
-
-def regroup(copy, grouped, rows):
-    copy(
-        out=grouped.rearrange("p (c i) t -> p c t i", i=4),
-        in_=rows.rearrange("p t (c i) -> p c t i", i=4),
-    )
 
 
 def tile_stc_cell_pa_kernel(tc, Gs, Xt, Ht_1, out_0, out_1):
@@ -86,150 +73,156 @@ def tile_stc_cell_pa_kernel(tc, Gs, Xt, Ht_1, out_0, out_1):
         x1_sb = keep.tile([P, TILES, FEATS], F32)
         x2_sb = keep.tile([P, TILES, FEATS], F32)
 
-        def flip_rows(g):
-            for pair in range(2):
-                for h in range(PASSES):
-                    flipped = psum.tile([P, 2, 2, P], F32, tag="bank")
-                    for i in range(2):
-                        words = (
-                            g_rows[:, PACK * g + 2 * pair + i, :]
-                            .bitcast(F32)
-                            .rearrange("p (h q u) -> p h u q", h=PASSES, u=2)
-                        )
-                        for u in range(2):
-                            nc.tensor.transpose(flipped[:, i, u, :], words[:, h, u, :], ident[:])
-                    first = (PACK * g + 2 * pair) * P * PACK
-                    nc.scalar.copy(
-                        out=left_grouped[:, h, first : first + 2 * P * PACK]
-                        .bitcast(F32)
-                        .rearrange("q (i p u) -> q i p u", i=2, u=2),
-                        in_=flipped[:].rearrange("q i u p -> q i p u"),
-                    )
+        V = nc.vector.tensor_copy
+        S = nc.scalar.copy
+        banks = {}
 
-        def quantise_left(g):
+        def quantise(grouped, codes, scales):
+            nc.vector.quantize_mx(out=codes.bitcast(FP8X4), scales=scales, in_=grouped)
+
+        def regroup(copy, grouped, rows):
+            copy(
+                out=grouped.rearrange("p (c i) t -> p c t i", i=4),
+                in_=rows.rearrange("p t (c i) -> p c t i", i=4),
+            )
+
+        def T(c):
             for h in range(PASSES):
-                quantise(
-                    nc,
-                    left_grouped[:, h, HALF * PACK * g : HALF * PACK * (g + 1)],
-                    left_codes[:, h, HALF * g : HALF * (g + 1)],
-                    left_scales[:, h, HALF * g : HALF * (g + 1)],
-                )
+                flipped = psum.tile([P, 2, 2, P], F32, tag="bank")
+                banks["T", c, h] = flipped
+                for i in range(2):
+                    words = g_rows[:, 2 * c + i, :].bitcast(F32).rearrange("p (h q u) -> p h u q", h=PASSES, u=2)
+                    for u in range(2):
+                        nc.tensor.transpose(flipped[:, i, u, :], words[:, h, u, :], ident[:])
 
-        def prepare_g(passes, quarters):
-            for h in passes:
-                for quarter in quarters:
-                    cols = slice(QUARTER * quarter, QUARTER * (quarter + 1))
-                    regroup(
-                        nc.scalar.copy if quarter == 3 else nc.vector.tensor_copy,
-                        g_grouped[:, h, cols, :],
-                        g_rows[:, PACK * h : PACK * (h + 1), cols],
-                    )
-            for h in passes:
-                for quarter in quarters:
-                    cols = slice(QUARTER * quarter, QUARTER * (quarter + 1))
-                    quantise(
-                        nc,
-                        g_grouped[:, h, cols, :].rearrange("p m t -> p (m t)"),
-                        g_codes[:, h, cols],
-                        g_scales[:, h, cols],
-                    )
-
-        def regroup_x(copy, s):
-            for g in range(PASSES):
-                regroup(
-                    copy,
-                    x_grouped[:, g, SOURCE_FEATS * s : SOURCE_FEATS * (s + 1), :],
-                    x_rows[:, s, g, :, :],
-                )
-
-        flip_rows(0)
-        prepare_g((0,), (0, 1))
-        quantise_left(0)
-        flip_rows(1)
-        prepare_g((1,), (0, 1))
-        prepare_g((0, 1), (2, 3))
-        quantise_left(1)
-        regroup_x(nc.scalar.copy, 0)
-
-        def product_windows(g, windows):
-            for w in windows:
-                cols = slice(P * w, P * (w + 1))
-                product = psum.tile([P, PACK, P], F32, tag="bank")
-                for t in range(PACK):
-                    rows = slice(P * (PACK * g + t), P * (PACK * g + t + 1))
-                    for h in range(PASSES):
-                        nc.tensor.matmul_mx(
-                            out=product[:, t, :],
-                            lhsT=left_codes[:, h, rows].bitcast(FP8X4),
-                            lhsT_scale=left_scales[:, h, rows],
-                            rhs=g_codes[:, h, cols].bitcast(FP8X4),
-                            rhs_scale=g_scales[:, h, cols],
-                            start=(h == 0),
-                            stop=(h == PASSES - 1),
-                        )
-                if w // PACK == g:
-                    nc.vector.scalar_tensor_tensor(
-                        out=t2_grouped[:, g, cols, :],
-                        in0=product[:].rearrange("p t m -> p m t"),
-                        scalar=2.0,
-                        in1=eye[:, P * (w % PACK) : P * (w % PACK + 1), :],
-                        op0=MULT,
-                        op1=SUBTRACT,
-                    )
-                else:
-                    nc.scalar.activation(
-                        out=t2_grouped[:, g, cols, :],
-                        in_=product[:].rearrange("p t m -> p m t"),
-                        func=COPY,
-                        scale=2.0,
-                    )
-
-        def quantise_t2(g, half):
-            cols = slice(HALF * half, HALF * (half + 1))
-            quantise(
-                nc,
-                t2_grouped[:, g, cols, :].rearrange("p m t -> p (m t)"),
-                t2_codes[:, g, cols],
-                t2_scales[:, g, cols],
+        def E(copy, c, h):
+            first = 2 * c * P * PACK
+            copy(
+                out=left_grouped[:, h, first : first + 2 * P * PACK].bitcast(F32).rearrange("q (i p u) -> q i p u", i=2, u=2),
+                in_=banks["T", c, h][:].rearrange("q i u p -> q i p u"),
             )
 
-        def diffuse(codes, scales, result, out, odd_copy):
-            out_view = out.rearrange("b (m p) c l -> p (b m) (c l)", p=P)
-            for m in range(TILES):
-                cols = slice(P * m, P * (m + 1))
-                acc = psum.tile([P, FEATS], F32, tag="bank")
-                for g in range(PASSES):
+        def QL(h, c, n=1):
+            a, b = 2 * c * P, 2 * (c + n) * P
+            quantise(left_grouped[:, h, PACK * a : PACK * b], left_codes[:, h, a:b], left_scales[:, h, a:b])
+
+        def IG(copy, h, w, n=2):
+            cols = slice(P * w, P * (w + n))
+            regroup(copy, g_grouped[:, h, cols, :], g_rows[:, PACK * h : PACK * (h + 1), cols])
+
+        def QG(h, w, n=2):
+            cols = slice(P * w, P * (w + n))
+            quantise(g_grouped[:, h, cols, :].rearrange("p m t -> p (m t)"), g_codes[:, h, cols], g_scales[:, h, cols])
+
+        def IX(copy, s, g):
+            regroup(copy, x_grouped[:, g, SOURCE_FEATS * s : SOURCE_FEATS * (s + 1), :], x_rows[:, s, g, :, :])
+
+        def QX(g):
+            quantise(x_grouped[:, g, :, :].rearrange("p f t -> p (f t)"), x_codes[:, g, :], x_scales[:, g, :])
+
+        def PR(g, w):
+            cols = slice(P * w, P * (w + 1))
+            product = psum.tile([P, PACK, P], F32, tag="bank")
+            banks["P", g, w] = product
+            for t in range(PACK):
+                rows = slice(P * (PACK * g + t), P * (PACK * g + t + 1))
+                for h in range(PASSES):
                     nc.tensor.matmul_mx(
-                        out=acc[:],
-                        lhsT=codes[:, g, cols].bitcast(FP8X4),
-                        lhsT_scale=scales[:, g, cols],
-                        rhs=x_codes[:, g, :].bitcast(FP8X4),
-                        rhs_scale=x_scales[:, g, :],
-                        start=(g == 0),
-                        stop=(g == PASSES - 1),
+                        out=product[:, t, :],
+                        lhsT=left_codes[:, h, rows].bitcast(FP8X4),
+                        lhsT_scale=left_scales[:, h, rows],
+                        rhs=g_codes[:, h, cols].bitcast(FP8X4),
+                        rhs_scale=g_scales[:, h, cols],
+                        start=(h == 0),
+                        stop=(h == PASSES - 1),
                     )
-                copy = odd_copy if m % 2 == 1 else nc.scalar.copy
-                copy(
-                    out=result[:, m, :].rearrange("p (c s l) -> p s c l", c=CHANNELS, s=2),
-                    in_=acc[:].rearrange("p (s c l) -> p s c l", s=2, c=CHANNELS),
-                )
-                nc.sync.dma_start(out=out_view[:, m, :], in_=result[:, m, :])
 
-        product_windows(0, range(TILES))
-        regroup_x(nc.vector.tensor_copy, 1)
-        for g in range(PASSES):
-            quantise(
-                nc,
-                x_grouped[:, g, :, :].rearrange("p f t -> p (f t)"),
-                x_codes[:, g, :],
-                x_scales[:, g, :],
+        def EP(g, w):
+            cols = slice(P * w, P * (w + 1))
+            product = banks["P", g, w]
+            if w // PACK == g:
+                nc.vector.scalar_tensor_tensor(
+                    out=t2_grouped[:, g, cols, :],
+                    in0=product[:].rearrange("p t m -> p m t"),
+                    scalar=2.0,
+                    in1=eye[:, P * (w % PACK) : P * (w % PACK + 1), :],
+                    op0=MULT,
+                    op1=SUBTRACT,
+                )
+            else:
+                nc.scalar.activation(
+                    out=t2_grouped[:, g, cols, :], in_=product[:].rearrange("p t m -> p m t"), func=COPY, scale=2.0
+                )
+
+        def QT(g, w, n=2):
+            cols = slice(P * w, P * (w + n))
+            quantise(t2_grouped[:, g, cols, :].rearrange("p m t -> p (m t)"), t2_codes[:, g, cols], t2_scales[:, g, cols])
+
+        def X(k, m):
+            codes, scales = ((g_codes, g_scales), (t2_codes, t2_scales))[k]
+            cols = slice(P * m, P * (m + 1))
+            acc = psum.tile([P, FEATS], F32, tag="bank")
+            banks["X", k, m] = acc
+            for g in range(PASSES):
+                nc.tensor.matmul_mx(
+                    out=acc[:],
+                    lhsT=codes[:, g, cols].bitcast(FP8X4),
+                    lhsT_scale=scales[:, g, cols],
+                    rhs=x_codes[:, g, :].bitcast(FP8X4),
+                    rhs_scale=x_scales[:, g, :],
+                    start=(g == 0),
+                    stop=(g == PASSES - 1),
+                )
+
+        def EX(copy, k, m):
+            result, out = ((x1_sb, out_0), (x2_sb, out_1))[k]
+            copy(
+                out=result[:, m, :].rearrange("p (c s l) -> p s c l", c=CHANNELS, s=2),
+                in_=banks["X", k, m][:].rearrange("p (s c l) -> p s c l", s=2, c=CHANNELS),
             )
-        quantise_t2(0, 0)
-        quantise_t2(0, 1)
-        product_windows(1, range(TILES // 2))
-        quantise_t2(1, 0)
-        product_windows(1, range(TILES // 2, TILES - WINDOWS_AFTER_X1))
-        diffuse(g_codes, g_scales, x1_sb, out_0, nc.scalar.copy)
-        product_windows(1, range(TILES - WINDOWS_AFTER_X1, TILES))
-        quantise_t2(1, 1)
-        diffuse(t2_codes, t2_scales, x2_sb, out_1, nc.vector.tensor_copy)
+            nc.sync.dma_start(out=out.rearrange("b (m p) c l -> p (b m) (c l)", p=P)[:, m, :], in_=result[:, m, :])
+
+        T(0); T(1)
+        E(S,0,0); E(S,0,1)
+        IG(V,0,0)
+        E(S,1,0); E(S,1,1)
+        QL(0,0); QL(1,0)
+        QG(0,0)
+        T(2); T(3)
+        QL(0,1); QL(1,1)
+        IG(S,0,2)
+        IG(V,1,0,1); IG(V,1,1,1); QG(1,0,1); QG(1,1,1)
+        PR(0,0); PR(0,1)
+        IG(V,1,2); QG(0,2); QG(1,2)
+        E(S,2,0); E(S,2,1); E(S,3,0); E(S,3,1)
+        PR(0,2); PR(0,3)
+        QL(0,2); QL(1,2); QL(0,3); QL(1,3)
+        IG(S,1,4)
+        PR(1,0); PR(1,1)
+        IG(V,0,4); EP(0,0); EP(0,1); QG(0,4); QG(1,4)
+        PR(1,2); PR(1,3)
+        EP(1,0); EP(1,1)
+        PR(0,4); PR(0,5)
+        EP(0,2); EP(0,3)
+        IG(S,0,6)
+        PR(1,4); PR(1,5)
+        IG(V,1,6); IX(V,1,0); QG(0,6); QG(1,6)
+        EP(1,2); EP(1,3)
+        PR(0,6); PR(0,7)
+        EP(0,4); EP(0,5)
+        IX(V,1,1); IX(V,0,0)
+        IX(S,0,1)
+        PR(1,6); PR(1,7)
+        QX(0); QX(1)
+        EP(0,6); EP(0,7)
+        EP(1,4); EP(1,5)
+        QT(0,0,4); QT(1,0,4)
+        for m in range(8):
+            X(0,m)
+            EX(S,0,m)
+            if m == 1:
+                EP(1,6); EP(1,7)
+            if m == 3:
+                QT(0,4,4); QT(1,4,4)
+        for m in range(8):
+            X(1,m); EX(V if m % 2 else S,1,m)

@@ -197,32 +197,48 @@ def tile_stc_cell_pa_kernel(tc, Gs, Xt, Ht_1, out_0, out_1):
         E(S,2,0); E(S,2,1); E(S,3,0); E(S,3,1)
         PR(0,2); PR(0,3)
         QL(0,2); QL(1,2); QL(0,3); QL(1,3)
-        IG(S,1,4)
+        IX(S,0,0); IX(S,0,1)
         PR(1,0); PR(1,1)
-        IG(V,0,4); EP(0,0); EP(0,1); QG(0,4); QG(1,4)
+        IX(V,1,0); IX(V,1,1)
+        QX(0)
+        EP(0,0)
+        QX(1)
+        EP(0,1)
         PR(1,2); PR(1,3)
         EP(1,0); EP(1,1)
-        PR(0,4); PR(0,5)
+        X(0,0); X(0,1)
         EP(0,2); EP(0,3)
-        IG(S,0,6)
-        PR(1,4); PR(1,5)
-        IG(V,1,6); IX(V,1,0); QG(0,6); QG(1,6)
+        QT(0,0); QT(1,0)
         EP(1,2); EP(1,3)
-        PR(0,6); PR(0,7)
+        X(0,2); X(0,3)
+        EX(S,0,0); EX(S,0,1)
+        QT(0,2); QT(1,2)
+        X(1,0); X(1,1)
+        IG(V,0,4); IG(V,1,4)
+        EX(S,0,2); EX(S,0,3)
+        X(1,2); X(1,3)
+        QG(0,4); QG(1,4)
+        EX(S,1,0); EX(V,1,1)
+        IG(V,0,6)
+        EX(S,1,2); EX(V,1,3)
+        PR(0,4); PR(0,5)
+        IG(S,1,6)
+        PR(1,4); PR(1,5)
+        QG(0,6)
         EP(0,4); EP(0,5)
-        IX(V,1,1); IX(V,0,0)
-        IX(S,0,1)
-        PR(1,6); PR(1,7)
-        QX(0); QX(1)
-        EP(0,6); EP(0,7)
+        QG(1,6)
+        X(0,4); X(0,5)
         EP(1,4); EP(1,5)
-        QT(0,0,4); QT(1,0,4)
-        for m in range(8):
-            X(0,m)
-            EX(S,0,m)
-            if m == 1:
-                EP(1,6); EP(1,7)
-            if m == 3:
-                QT(0,4,4); QT(1,4,4)
-        for m in range(8):
-            X(1,m); EX(V if m % 2 else S,1,m)
+        PR(0,6); PR(0,7)
+        EX(S,0,4); EX(S,0,5)
+        QT(0,4); QT(1,4)
+        PR(1,6); PR(1,7)
+        EP(0,6); EP(0,7)
+        X(1,4); X(1,5)
+        EP(1,6); EP(1,7)
+        X(0,6); X(0,7)
+        EX(S,1,4); EX(S,1,5)
+        QT(0,6); QT(1,6)
+        X(1,6); X(1,7)
+        EX(V,0,6); EX(S,0,7)
+        EX(V,1,6); EX(S,1,7)

@@ -232,13 +232,13 @@ def tile_stc_cell_pa_kernel(tc, Gs, Xt, Ht_1, out_0, out_1):
         PR(0,6); PR(0,7)
         EX(S,0,4); EX(S,0,5)
         QT(0,4); QT(1,4)
-        PR(1,6); PR(1,7)
-        EP(0,6); EP(0,7)
         X(1,4); X(1,5)
-        EP(1,6); EP(1,7)
+        EP(0,6); EP(0,7)
+        PR(1,6); PR(1,7)
+        QT(0,6)
+        EX(S,1,4); EX(V,1,5)
         X(0,6); X(0,7)
-        EX(S,1,4); EX(S,1,5)
-        QT(0,6); QT(1,6)
+        EP(1,6); QT(1,6,1); EP(1,7); QT(1,7,1)
+        EX(S,0,6); EX(S,0,7)
         X(1,6); X(1,7)
-        EX(V,0,6); EX(S,0,7)
         EX(V,1,6); EX(S,1,7)

@@ -82,8 +82,8 @@ def tile_stc_cell_pa_kernel(tc, Gs, Xt, Ht_1, out_0, out_1):
 
         def regroup(copy, grouped, rows):
             copy(
-                out=grouped.rearrange("p (c i) t -> p c t i", i=4),
-                in_=rows.rearrange("p t (c i) -> p c t i", i=4),
+                out=grouped.rearrange("p (c i) t -> p c t i", i=8),
+                in_=rows.rearrange("p t (c i) -> p c t i", i=8),
             )
 
         def T(c):

@@ -210,19 +210,20 @@ def tile_stc_cell_pa_kernel(tc, Gs, Xt, Ht_1, out_0, out_1):
         EP(0,2); EP(0,3)
         QT(0,0); QT(1,0)
         EP(1,2); EP(1,3)
+        IG(S,1,4)
         X(0,2); X(0,3)
         EX(S,0,0); EX(S,0,1)
         QT(0,2); QT(1,2)
         X(1,0); X(1,1)
-        IG(V,0,4); IG(V,1,4)
+        IG(V,0,4)
         EX(S,0,2); EX(S,0,3)
         X(1,2); X(1,3)
-        QG(0,4); QG(1,4)
+        QG(1,4); QG(0,4)
         EX(S,1,0); EX(V,1,1)
         IG(V,0,6)
         EX(S,1,2); EX(V,1,3)
         PR(0,4); PR(0,5)
-        IG(S,1,6)
+        IG(V,1,6)
         PR(1,4); PR(1,5)
         QG(0,6)
         EP(0,4); EP(0,5)

@@ -182,6 +182,31 @@ def tile_stc_cell_pa_kernel(tc, Gs, Xt, Ht_1, out_0, out_1):
             )
             nc.sync.dma_start(out=out.rearrange("b (m p) c l -> p (b m) (c l)", p=P)[:, m, :], in_=result[:, m, :])
 
+        def XL(k, m):
+            codes, scales = ((g_codes, g_scales), (t2_codes, t2_scales))[k]
+            result, out = ((x1_sb, out_0), (x2_sb, out_1))[k]
+            cols = slice(P * m, P * (m + 1))
+            for pair, copy in enumerate((V, S)):
+                acc = psum.tile([P, 2, P], F32, tag="bank")
+                for s in range(2):
+                    feats = slice(SOURCE_FEATS * s + P * pair, SOURCE_FEATS * s + P * (pair + 1))
+                    for g in range(PASSES):
+                        nc.tensor.matmul_mx(
+                            out=acc[:, s, :],
+                            lhsT=codes[:, g, cols].bitcast(FP8X4),
+                            lhsT_scale=scales[:, g, cols],
+                            rhs=x_codes[:, g, feats].bitcast(FP8X4),
+                            rhs_scale=x_scales[:, g, feats],
+                            start=(g == 0),
+                            stop=(g == PASSES - 1),
+                        )
+                part = slice(2 * P * pair, 2 * P * (pair + 1))
+                copy(
+                    out=result[:, m, part].rearrange("p (c s l) -> p s c l", c=2, s=2),
+                    in_=acc[:].rearrange("p s (c l) -> p s c l", c=2),
+                )
+                nc.sync.dma_start(out=out.rearrange("b (m p) c l -> p (b m) (c l)", p=P)[:, m, part], in_=result[:, m, part])
+
         T(0); T(1)
         E(S,0,0); E(S,0,1)
         IG(V,0,0)
@@ -210,13 +235,12 @@ def tile_stc_cell_pa_kernel(tc, Gs, Xt, Ht_1, out_0, out_1):
         EP(0,2); EP(0,3)
         QT(0,0); QT(1,0)
         EP(1,2); EP(1,3)
-        IG(S,1,4)
+        IG(S,1,4); IG(S,0,4)
         X(0,2); X(0,3)
         EX(S,0,0); EX(S,0,1)
         QT(0,2); QT(1,2)
         X(1,0); X(1,1)
-        IG(V,0,4)
-        EX(S,0,2); EX(S,0,3)
+        EX(V,0,2); EX(S,0,3)
         X(1,2); X(1,3)
         QG(1,4); QG(0,4)
         EX(S,1,0); EX(V,1,1)
@@ -241,5 +265,6 @@ def tile_stc_cell_pa_kernel(tc, Gs, Xt, Ht_1, out_0, out_1):
         X(0,6); X(0,7)
         EP(1,6); QT(1,6,1); EP(1,7); QT(1,7,1)
         EX(S,0,6); EX(S,0,7)
-        X(1,6); X(1,7)
-        EX(V,1,6); EX(S,1,7)
+        X(1,6)
+        EX(V,1,6)
+        XL(1,7)

@@ -263,7 +263,7 @@ def tile_stc_cell_pa_kernel(tc, Gs, Xt, Ht_1, out_0, out_1):
         QT(0,6)
         EX(S,1,4); EX(V,1,5)
         X(0,6); X(0,7)
-        EP(1,6); QT(1,6,1); EP(1,7); QT(1,7,1)
+        EP(1,6); EP(1,7); QT(1,6,1); QT(1,7,1)
         EX(S,0,6); EX(S,0,7)
         X(1,6)
         EX(V,1,6)

@@ -35,28 +35,31 @@ def tile_stc_cell_pa_kernel(tc, Gs, Xt, Ht_1, out_0, out_1):
         stack.enter_context(tc.manual_schedule())
 
         g_rows = keep.tile([P, PASSES * PACK, NODES], BF16)
-        g_dram = Gs.rearrange("(g p t) m -> g p t m", g=PASSES, t=PACK)
+        g_dram = Gs.rearrange("(c p e) m -> c p e m", p=P, e=2)
         for g in range(PASSES):
             for pair in range(2):
                 nc.sync.dma_start(
                     out=g_rows[:, PACK * g + 2 * pair : PACK * g + 2 * pair + 2, :],
-                    in_=g_dram[g][:, 2 * pair : 2 * pair + 2, :],
+                    in_=g_dram[2 * g + pair],
                 )
         x_rows = keep.tile([P, 2, PASSES, PACK, SOURCE_FEATS], BF16)
         for s, source in enumerate((Xt, Ht_1)):
             nc.sync.dma_start(
-                out=x_rows[:, s, :, :, :].rearrange("p g t f -> p g (t f)"),
-                in_=source.rearrange("b (g p t) c l -> p (b g) (t c l)", g=PASSES, t=PACK),
+                out=x_rows[:, s, :, :, :].rearrange("p g (u e) f -> p (g u) (e f)", e=2),
+                in_=source.rearrange("b (k p e) c l -> p (b k) (e c l)", p=P, e=2),
             )
 
+        zeros = keep.tile([P, K_PASS], BF16)
+        nc.vector.memset(zeros[:], 0.0)
         ident = keep.tile([P, P], F32)
         make_identity(nc, ident[:])
         eye = keep.tile([P, K_PASS, PACK], BF16)
         nc.vector.memset(eye[:], 0.0)
-        nc.vector.tensor_copy(
-            out=eye[:].rearrange("p (q a) t -> p q (a t)", a=PACK)[:, :, 0 : PACK * PACK : PACK + 1],
-            in_=ident[:].unsqueeze(2).to_broadcast([P, P, PACK]),
-        )
+        for u in range(2):
+            nc.vector.tensor_copy(
+                out=eye[:].rearrange("p (u q e) t -> p u q (e t)", u=2, e=2)[:, u, :, 2 * u : 2 * u + PACK + 2 : PACK + 1],
+                in_=ident[:].unsqueeze(2).to_broadcast([P, P, 2]),
+            )
 
         left_grouped = keep.tile([P, PASSES, NODES * PACK], BF16, align_bytes=64)
         left_codes = keep.tile([P, PASSES, NODES], U32, align_bytes=64)
@@ -91,9 +94,14 @@ def tile_stc_cell_pa_kernel(tc, Gs, Xt, Ht_1, out_0, out_1):
                 flipped = psum.tile([P, 2, 2, P], F32, tag="bank")
                 banks["T", c, h] = flipped
                 for i in range(2):
-                    words = g_rows[:, 2 * c + i, :].bitcast(F32).rearrange("p (h q u) -> p h u q", h=PASSES, u=2)
+                    words = g_rows[:, 2 * c + i, :].bitcast(F32).rearrange("p (h u q) -> p h u q", h=PASSES, u=2)
                     for u in range(2):
                         nc.tensor.transpose(flipped[:, i, u, :], words[:, h, u, :], ident[:])
+
+        def W(n):
+            idle = psum.tile([P, K_PASS], F32, tag="bank")
+            for i in range(n):
+                nc.tensor.matmul(out=idle[:], lhsT=zeros[:, 0:P], rhs=zeros[:], start=True, stop=True)
 
         def E(copy, c, h):
             first = 2 * c * P * PACK
@@ -207,13 +215,16 @@ def tile_stc_cell_pa_kernel(tc, Gs, Xt, Ht_1, out_0, out_1):
                 )
                 nc.sync.dma_start(out=out.rearrange("b (m p) c l -> p (b m) (c l)", p=P)[:, m, part], in_=result[:, m, part])
 
-        T(0); T(1)
+        W(2)
+        T(0); W(1)
+        T(1); W(2)
         E(S,0,0); E(S,0,1)
         IG(V,0,0)
         E(S,1,0); E(S,1,1)
         QL(0,0); QL(1,0)
         QG(0,0)
-        T(2); T(3)
+        T(2); W(2)
+        T(3)
         QL(0,1); QL(1,1)
         IG(S,0,2)
         IG(V,1,0,1); IG(V,1,1,1); QG(1,0,1); QG(1,1,1)

@@ -50,7 +50,7 @@ def tile_stc_cell_pa_kernel(tc, Gs, Xt, Ht_1, out_0, out_1):
             )
 
         zeros = keep.tile([P, K_PASS], BF16)
-        nc.vector.memset(zeros[:], 0.0)
+        nc.vector.memset(zeros[:].bitcast(U32), 0)
         ident = keep.tile([P, P], F32)
         make_identity(nc, ident[:])
         eye = keep.tile([P, K_PASS, PACK], BF16)
@@ -215,7 +215,7 @@ def tile_stc_cell_pa_kernel(tc, Gs, Xt, Ht_1, out_0, out_1):
                 )
                 nc.sync.dma_start(out=out.rearrange("b (m p) c l -> p (b m) (c l)", p=P)[:, m, part], in_=result[:, m, part])
 
-        W(2)
+        W(4)
         T(0); W(1)
         T(1); W(2)
         E(S,0,0); E(S,0,1)
@@ -223,7 +223,7 @@ def tile_stc_cell_pa_kernel(tc, Gs, Xt, Ht_1, out_0, out_1):
         E(S,1,0); E(S,1,1)
         QL(0,0); QL(1,0)
         QG(0,0)
-        T(2); W(2)
+        T(2); W(1)
         T(3)
         QL(0,1); QL(1,1)
         IG(S,0,2)

@@ -18,11 +18,11 @@ K_PASS = P * PACK
 NODES = 1024
 PASSES = NODES // K_PASS
 TILES = NODES // P
+PAIRS = TILES // 2
 CHANNELS = 4
 HALF_FEATS = 64
 SOURCE_FEATS = CHANNELS * HALF_FEATS
 FEATS = 2 * SOURCE_FEATS
-QUARTER = NODES // 4
 
 FLOPS = 2 * NODES * NODES * NODES + 2 * 2 * NODES * NODES * FEATS
 
@@ -36,12 +36,10 @@ def tile_stc_cell_pa_kernel(tc, Gs, Xt, Ht_1, out_0, out_1):
 
         g_rows = keep.tile([P, PASSES * PACK, NODES], BF16)
         g_dram = Gs.rearrange("(c p e) m -> c p e m", p=P, e=2)
-        for g in range(PASSES):
-            for pair in range(2):
-                nc.sync.dma_start(
-                    out=g_rows[:, PACK * g + 2 * pair : PACK * g + 2 * pair + 2, :],
-                    in_=g_dram[2 * g + pair],
-                )
+        for i in range(PACK):
+            nc.sync.dma_start(out=g_rows[:, i, :], in_=g_dram[i // 2][:, i % 2, :])
+        for c in range(2, 4):
+            nc.sync.dma_start(out=g_rows[:, 2 * c : 2 * c + 2, :], in_=g_dram[c])
         x_rows = keep.tile([P, 2, PASSES, PACK, SOURCE_FEATS], BF16)
         for s, source in enumerate((Xt, Ht_1)):
             nc.sync.dma_start(
@@ -61,15 +59,15 @@ def tile_stc_cell_pa_kernel(tc, Gs, Xt, Ht_1, out_0, out_1):
                 in_=ident[:].unsqueeze(2).to_broadcast([P, P, 2]),
             )
 
-        left_grouped = keep.tile([P, PASSES, NODES * PACK], BF16, align_bytes=64)
-        left_codes = keep.tile([P, PASSES, NODES], U32, align_bytes=64)
-        left_scales = keep.tile([P, PASSES, NODES], U8, align_bytes=64)
-        g_grouped = keep.tile([P, PASSES, NODES, PACK], BF16, align_bytes=64)
-        g_codes = keep.tile([P, PASSES, NODES], U32, align_bytes=64)
-        g_scales = keep.tile([P, PASSES, NODES], U8, align_bytes=64)
-        t2_grouped = keep.tile([P, PASSES, NODES, PACK], BF16, align_bytes=64)
-        t2_codes = keep.tile([P, PASSES, NODES], U32, align_bytes=64)
-        t2_scales = keep.tile([P, PASSES, NODES], U8, align_bytes=64)
+        left_grouped = keep.tile([P, PAIRS, PASSES, 2 * P * PACK], BF16, align_bytes=64)
+        left_codes = keep.tile([P, PAIRS, PASSES, 2 * P], U32, align_bytes=64)
+        left_scales = keep.tile([P, PAIRS, PASSES, 2 * P], U8, align_bytes=64)
+        g_grouped = keep.tile([P, PAIRS, PASSES, 2 * P, PACK], BF16, align_bytes=64)
+        g_codes = keep.tile([P, PAIRS, PASSES, 2 * P], U32, align_bytes=64)
+        g_scales = keep.tile([P, PAIRS, PASSES, 2 * P], U8, align_bytes=64)
+        t2_grouped = keep.tile([P, PAIRS, PASSES, 2 * P, PACK], BF16, align_bytes=64)
+        t2_codes = keep.tile([P, PAIRS, PASSES, 2 * P], U32, align_bytes=64)
+        t2_scales = keep.tile([P, PAIRS, PASSES, 2 * P], U8, align_bytes=64)
         x_grouped = keep.tile([P, PASSES, FEATS, PACK], BF16, align_bytes=64)
         x_codes = keep.tile([P, PASSES, FEATS], U32, align_bytes=64)
         x_scales = keep.tile([P, PASSES, FEATS], U8, align_bytes=64)
@@ -83,10 +81,42 @@ def tile_stc_cell_pa_kernel(tc, Gs, Xt, Ht_1, out_0, out_1):
         def quantise(grouped, codes, scales):
             nc.vector.quantize_mx(out=codes.bitcast(FP8X4), scales=scales, in_=grouped)
 
+        def both_passes(grouped, codes, scales, j):
+            flat = grouped[:, j, :, :] if len(grouped.shape) == 4 else grouped[:, j, :, :, :].rearrange("p h m t -> p h (m t)")
+            quantise(
+                flat.rearrange("p h n -> p (h n)"),
+                codes[:, j, :, :].rearrange("p h n -> p (h n)"),
+                scales[:, j, :, :].rearrange("p h n -> p (h n)"),
+            )
+
+        def one_pass(grouped, codes, scales, h, w, n):
+            cols = slice(P * (w % 2), P * (w % 2 + n))
+            quantise(grouped[:, w // 2, h, cols, :].rearrange("p m t -> p (m t)"), codes[:, w // 2, h, cols], scales[:, w // 2, h, cols])
+
         def regroup(copy, grouped, rows):
             copy(
                 out=grouped.rearrange("p (c i) t -> p c t i", i=8),
                 in_=rows.rearrange("p t (c i) -> p c t i", i=8),
+            )
+
+        def W(n):
+            idle = psum.tile([P, K_PASS], F32, tag="bank")
+            for i in range(n):
+                nc.tensor.matmul(out=idle[:], lhsT=zeros[:, 0:P], rhs=zeros[:], start=True, stop=True)
+
+        def T1(i):
+            flipped = psum.tile([P, 2, 2, P], F32, tag="bank")
+            banks["T1", i] = flipped
+            words = g_rows[:, i, :].bitcast(F32).rearrange("p (h u q) -> p h u q", h=PASSES, u=2)
+            for h in range(PASSES):
+                for u in range(2):
+                    nc.tensor.transpose(flipped[:, h, u, :], words[:, h, u, :], ident[:])
+
+        def E1(copy, i):
+            first = (i % 2) * P * PACK
+            copy(
+                out=left_grouped[:, i // 2, :, first : first + P * PACK].bitcast(F32).rearrange("q h (p u) -> q h p u", u=2),
+                in_=banks["T1", i][:].rearrange("q h u p -> q h p u"),
             )
 
         def T(c):
@@ -98,29 +128,24 @@ def tile_stc_cell_pa_kernel(tc, Gs, Xt, Ht_1, out_0, out_1):
                     for u in range(2):
                         nc.tensor.transpose(flipped[:, i, u, :], words[:, h, u, :], ident[:])
 
-        def W(n):
-            idle = psum.tile([P, K_PASS], F32, tag="bank")
-            for i in range(n):
-                nc.tensor.matmul(out=idle[:], lhsT=zeros[:, 0:P], rhs=zeros[:], start=True, stop=True)
-
         def E(copy, c, h):
-            first = 2 * c * P * PACK
             copy(
-                out=left_grouped[:, h, first : first + 2 * P * PACK].bitcast(F32).rearrange("q (i p u) -> q i p u", i=2, u=2),
+                out=left_grouped[:, c, h, :].bitcast(F32).rearrange("q (i p u) -> q i p u", i=2, u=2),
                 in_=banks["T", c, h][:].rearrange("q i u p -> q i p u"),
             )
 
-        def QL(h, c, n=1):
-            a, b = 2 * c * P, 2 * (c + n) * P
-            quantise(left_grouped[:, h, PACK * a : PACK * b], left_codes[:, h, a:b], left_scales[:, h, a:b])
+        def QL(c):
+            both_passes(left_grouped, left_codes, left_scales, c)
 
         def IG(copy, h, w, n=2):
-            cols = slice(P * w, P * (w + n))
-            regroup(copy, g_grouped[:, h, cols, :], g_rows[:, PACK * h : PACK * (h + 1), cols])
+            cols = slice(P * (w % 2), P * (w % 2 + n))
+            regroup(copy, g_grouped[:, w // 2, h, cols, :], g_rows[:, PACK * h : PACK * (h + 1), P * w : P * (w + n)])
 
         def QG(h, w, n=2):
-            cols = slice(P * w, P * (w + n))
-            quantise(g_grouped[:, h, cols, :].rearrange("p m t -> p (m t)"), g_codes[:, h, cols], g_scales[:, h, cols])
+            one_pass(g_grouped, g_codes, g_scales, h, w, n)
+
+        def QGG(w):
+            both_passes(g_grouped, g_codes, g_scales, w // 2)
 
         def IX(copy, s, g):
             regroup(copy, x_grouped[:, g, SOURCE_FEATS * s : SOURCE_FEATS * (s + 1), :], x_rows[:, s, g, :, :])
@@ -128,29 +153,37 @@ def tile_stc_cell_pa_kernel(tc, Gs, Xt, Ht_1, out_0, out_1):
         def QX(g):
             quantise(x_grouped[:, g, :, :].rearrange("p f t -> p (f t)"), x_codes[:, g, :], x_scales[:, g, :])
 
+        def QXX():
+            quantise(
+                x_grouped[:].rearrange("p g f t -> p (g f t)"),
+                x_codes[:].rearrange("p g f -> p (g f)"),
+                x_scales[:].rearrange("p g f -> p (g f)"),
+            )
+
         def PR(g, w):
-            cols = slice(P * w, P * (w + 1))
+            cols = slice(P * (w % 2), P * (w % 2 + 1))
             product = psum.tile([P, PACK, P], F32, tag="bank")
             banks["P", g, w] = product
             for t in range(PACK):
-                rows = slice(P * (PACK * g + t), P * (PACK * g + t + 1))
+                j = 2 * g + t // 2
+                rows = slice(P * (t % 2), P * (t % 2 + 1))
                 for h in range(PASSES):
                     nc.tensor.matmul_mx(
                         out=product[:, t, :],
-                        lhsT=left_codes[:, h, rows].bitcast(FP8X4),
-                        lhsT_scale=left_scales[:, h, rows],
-                        rhs=g_codes[:, h, cols].bitcast(FP8X4),
-                        rhs_scale=g_scales[:, h, cols],
+                        lhsT=left_codes[:, j, h, rows].bitcast(FP8X4),
+                        lhsT_scale=left_scales[:, j, h, rows],
+                        rhs=g_codes[:, w // 2, h, cols].bitcast(FP8X4),
+                        rhs_scale=g_scales[:, w // 2, h, cols],
                         start=(h == 0),
                         stop=(h == PASSES - 1),
                     )
 
         def EP(g, w):
-            cols = slice(P * w, P * (w + 1))
+            cols = slice(P * (w % 2), P * (w % 2 + 1))
             product = banks["P", g, w]
             if w // PACK == g:
                 nc.vector.scalar_tensor_tensor(
-                    out=t2_grouped[:, g, cols, :],
+                    out=t2_grouped[:, w // 2, g, cols, :],
                     in0=product[:].rearrange("p t m -> p m t"),
                     scalar=2.0,
                     in1=eye[:, P * (w % PACK) : P * (w % PACK + 1), :],
@@ -159,23 +192,35 @@ def tile_stc_cell_pa_kernel(tc, Gs, Xt, Ht_1, out_0, out_1):
                 )
             else:
                 nc.scalar.activation(
-                    out=t2_grouped[:, g, cols, :], in_=product[:].rearrange("p t m -> p m t"), func=COPY, scale=2.0
+                    out=t2_grouped[:, w // 2, g, cols, :], in_=product[:].rearrange("p t m -> p m t"), func=COPY, scale=2.0
                 )
 
+        def EPV(g, w):
+            cols = slice(P * (w % 2), P * (w % 2 + 1))
+            nc.vector.tensor_scalar(
+                out=t2_grouped[:, w // 2, g, cols, :],
+                in0=banks["P", g, w][:].rearrange("p t m -> p m t"),
+                scalar1=2.0,
+                scalar2=None,
+                op0=MULT,
+            )
+
         def QT(g, w, n=2):
-            cols = slice(P * w, P * (w + n))
-            quantise(t2_grouped[:, g, cols, :].rearrange("p m t -> p (m t)"), t2_codes[:, g, cols], t2_scales[:, g, cols])
+            one_pass(t2_grouped, t2_codes, t2_scales, g, w, n)
+
+        def QTT(w):
+            both_passes(t2_grouped, t2_codes, t2_scales, w // 2)
 
         def X(k, m):
             codes, scales = ((g_codes, g_scales), (t2_codes, t2_scales))[k]
-            cols = slice(P * m, P * (m + 1))
+            cols = slice(P * (m % 2), P * (m % 2 + 1))
             acc = psum.tile([P, FEATS], F32, tag="bank")
             banks["X", k, m] = acc
             for g in range(PASSES):
                 nc.tensor.matmul_mx(
                     out=acc[:],
-                    lhsT=codes[:, g, cols].bitcast(FP8X4),
-                    lhsT_scale=scales[:, g, cols],
+                    lhsT=codes[:, m // 2, g, cols].bitcast(FP8X4),
+                    lhsT_scale=scales[:, m // 2, g, cols],
                     rhs=x_codes[:, g, :].bitcast(FP8X4),
                     rhs_scale=x_scales[:, g, :],
                     start=(g == 0),
@@ -193,7 +238,7 @@ def tile_stc_cell_pa_kernel(tc, Gs, Xt, Ht_1, out_0, out_1):
         def XL(k, m):
             codes, scales = ((g_codes, g_scales), (t2_codes, t2_scales))[k]
             result, out = ((x1_sb, out_0), (x2_sb, out_1))[k]
-            cols = slice(P * m, P * (m + 1))
+            cols = slice(P * (m % 2), P * (m % 2 + 1))
             for pair, copy in enumerate((V, S)):
                 acc = psum.tile([P, 2, P], F32, tag="bank")
                 for s in range(2):
@@ -201,8 +246,8 @@ def tile_stc_cell_pa_kernel(tc, Gs, Xt, Ht_1, out_0, out_1):
                     for g in range(PASSES):
                         nc.tensor.matmul_mx(
                             out=acc[:, s, :],
-                            lhsT=codes[:, g, cols].bitcast(FP8X4),
-                            lhsT_scale=scales[:, g, cols],
+                            lhsT=codes[:, m // 2, g, cols].bitcast(FP8X4),
+                            lhsT_scale=scales[:, m // 2, g, cols],
                             rhs=x_codes[:, g, feats].bitcast(FP8X4),
                             rhs_scale=x_scales[:, g, feats],
                             start=(g == 0),
@@ -215,67 +260,62 @@ def tile_stc_cell_pa_kernel(tc, Gs, Xt, Ht_1, out_0, out_1):
                 )
                 nc.sync.dma_start(out=out.rearrange("b (m p) c l -> p (b m) (c l)", p=P)[:, m, part], in_=result[:, m, part])
 
-        W(4)
-        T(0); W(1)
-        T(1); W(2)
-        E(S,0,0); E(S,0,1)
-        IG(V,0,0)
-        E(S,1,0); E(S,1,1)
-        QL(0,0); QL(1,0)
-        QG(0,0)
+        W(3)
+        T1(0); T1(1); W(1); T1(2); T1(3); W(2)
+        E1(S,0); E1(S,1); E1(S,2); E1(S,3)
+        IG(V,0,4)
+        QL(0)
+        QG(0,4)
         T(2); W(1)
         T(3)
-        QL(0,1); QL(1,1)
-        IG(S,0,2)
-        IG(V,1,0,1); IG(V,1,1,1); QG(1,0,1); QG(1,1,1)
-        PR(0,0); PR(0,1)
-        IG(V,1,2); QG(0,2); QG(1,2)
-        E(S,2,0); E(S,2,1); E(S,3,0); E(S,3,1)
-        PR(0,2); PR(0,3)
-        QL(0,2); QL(1,2); QL(0,3); QL(1,3)
-        IX(S,0,0); IX(S,0,1)
-        PR(1,0); PR(1,1)
-        IX(V,1,0); IX(V,1,1)
-        QX(0)
-        EP(0,0)
-        QX(1)
-        EP(0,1)
-        PR(1,2); PR(1,3)
-        EP(1,0); EP(1,1)
-        X(0,0); X(0,1)
-        EP(0,2); EP(0,3)
-        QT(0,0); QT(1,0)
-        EP(1,2); EP(1,3)
-        IG(S,1,4); IG(S,0,4)
-        X(0,2); X(0,3)
-        EX(S,0,0); EX(S,0,1)
-        QT(0,2); QT(1,2)
-        X(1,0); X(1,1)
-        EX(V,0,2); EX(S,0,3)
-        X(1,2); X(1,3)
-        QG(1,4); QG(0,4)
-        EX(S,1,0); EX(V,1,1)
-        IG(V,0,6)
-        EX(S,1,2); EX(V,1,3)
+        QL(1)
+        IG(S,0,6)
+        IG(V,1,4,1); IG(V,1,5,1); QG(1,4,1); QG(1,5,1)
         PR(0,4); PR(0,5)
-        IG(V,1,6)
-        PR(1,4); PR(1,5)
-        QG(0,6)
-        EP(0,4); EP(0,5)
-        QG(1,6)
-        X(0,4); X(0,5)
-        EP(1,4); EP(1,5)
+        IG(V,1,6); QG(0,6); QG(1,6)
+        E(S,2,0); E(S,2,1); E(S,3,0); E(S,3,1)
         PR(0,6); PR(0,7)
-        EX(S,0,4); EX(S,0,5)
-        QT(0,4); QT(1,4)
-        X(1,4); X(1,5)
-        EP(0,6); EP(0,7)
+        QL(2); QL(3)
+        IX(S,0,0); IX(S,0,1)
+        PR(1,4); PR(1,5)
+        IX(V,1,0); IX(V,1,1)
+        QX(0); QX(1)
+        EP(0,4); EP(0,5)
         PR(1,6); PR(1,7)
-        QT(0,6)
-        EX(S,1,4); EX(V,1,5)
+        EP(0,6); EP(0,7)
+        EP(1,4)
+        X(0,4); X(0,5)
+        EP(1,5)
+        QT(0,4); QT(1,4)
+        EP(1,6); EP(1,7)
+        IG(S,1,0); IG(S,0,0)
         X(0,6); X(0,7)
-        EP(1,6); EP(1,7); QT(1,6,1); QT(1,7,1)
+        QT(0,6); QT(1,6)
+        X(1,4); X(1,5)
+        EX(S,0,4); EX(S,0,5)
+        QG(1,0); QG(0,0)
+        X(1,6); X(1,7)
         EX(S,0,6); EX(S,0,7)
-        X(1,6)
-        EX(V,1,6)
-        XL(1,7)
+        IG(V,0,2); IG(V,1,2)
+        PR(0,0); PR(0,1)
+        EX(S,1,4); EX(V,1,5)
+        QG(0,2); QG(1,2)
+        PR(1,0); PR(1,1)
+        EX(S,1,6); EX(V,1,7)
+        EP(0,0); EP(0,1)
+        X(0,0); X(0,1)
+        EP(1,0); EP(1,1)
+        QT(1,0); QT(0,0)
+        PR(0,2); PR(0,3)
+        EX(S,0,0); EX(S,0,1)
+        X(1,0); X(1,1)
+        EP(0,2); EP(0,3)
+        PR(1,2); PR(1,3)
+        EX(S,1,0); EX(V,1,1)
+        X(0,2); X(0,3)
+        EP(1,2); EPV(1,3)
+        QT(0,2); QT(1,2)
+        EX(S,0,2); EX(S,0,3)
+        X(1,2)
+        EX(V,1,2)
+        XL(1,3)

@@ -36,9 +36,7 @@ def tile_stc_cell_pa_kernel(tc, Gs, Xt, Ht_1, out_0, out_1):
 
         g_rows = keep.tile([P, PASSES * PACK, NODES], BF16)
         g_dram = Gs.rearrange("(c p e) m -> c p e m", p=P, e=2)
-        for i in range(PACK):
-            nc.sync.dma_start(out=g_rows[:, i, :], in_=g_dram[i // 2][:, i % 2, :])
-        for c in range(2, 4):
+        for c in range(4):
             nc.sync.dma_start(out=g_rows[:, 2 * c : 2 * c + 2, :], in_=g_dram[c])
         x_rows = keep.tile([P, 2, PASSES, PACK, SOURCE_FEATS], BF16)
         for s, source in enumerate((Xt, Ht_1)):
@@ -136,6 +134,9 @@ def tile_stc_cell_pa_kernel(tc, Gs, Xt, Ht_1, out_0, out_1):
 
         def QL(c):
             both_passes(left_grouped, left_codes, left_scales, c)
+
+        def QLH(c, h):
+            quantise(left_grouped[:, c, h, :], left_codes[:, c, h, :], left_scales[:, c, h, :])
 
         def IG(copy, h, w, n=2):
             cols = slice(P * (w % 2), P * (w % 2 + n))
@@ -260,22 +261,22 @@ def tile_stc_cell_pa_kernel(tc, Gs, Xt, Ht_1, out_0, out_1):
                 )
                 nc.sync.dma_start(out=out.rearrange("b (m p) c l -> p (b m) (c l)", p=P)[:, m, part], in_=result[:, m, part])
 
-        W(3)
-        T1(0); T1(1); W(1); T1(2); T1(3); W(2)
-        E1(S,0); E1(S,1); E1(S,2); E1(S,3)
+        W(4)
+        T(0); W(1)
+        T(1); W(2)
+        E(S,0,0); E(S,0,1); E(S,1,0); E(S,1,1)
         IG(V,0,4)
-        QL(0)
-        QG(0,4)
+        QLH(0,0); QG(0,4); QLH(0,1)
         T(2); W(1)
         T(3)
-        QL(1)
+        QLH(1,0); QLH(1,1)
         IG(S,0,6)
         IG(V,1,4,1); IG(V,1,5,1); QG(1,4,1); QG(1,5,1)
         PR(0,4); PR(0,5)
         IG(V,1,6); QG(0,6); QG(1,6)
         E(S,2,0); E(S,2,1); E(S,3,0); E(S,3,1)
         PR(0,6); PR(0,7)
-        QL(2); QL(3)
+        QLH(2,0); QLH(2,1); QLH(3,0); QLH(3,1)
         IX(S,0,0); IX(S,0,1)
         PR(1,4); PR(1,5)
         IX(V,1,0); IX(V,1,1)

@@ -259,7 +259,7 @@ def tile_stc_cell_pa_kernel(tc, Gs, Xt, Ht_1, out_0, out_1):
                     out=result[:, m, part].rearrange("p (c s l) -> p s c l", c=2, s=2),
                     in_=acc[:].rearrange("p s (c l) -> p s c l", c=2),
                 )
-                nc.sync.dma_start(out=out.rearrange("b (m p) c l -> p (b m) (c l)", p=P)[:, m, part], in_=result[:, m, part])
+            nc.sync.dma_start(out=out.rearrange("b (m p) c l -> p (b m) (c l)", p=P)[:, m, :], in_=result[:, m, :])
 
         W(4)
         T(0); W(1)
@@ -307,16 +307,18 @@ def tile_stc_cell_pa_kernel(tc, Gs, Xt, Ht_1, out_0, out_1):
         X(0,0); X(0,1)
         EP(1,0); EP(1,1)
         QT(1,0); QT(0,0)
-        PR(0,2); PR(0,3)
+        PR(0,2); PR(1,2)
         EX(S,0,0); EX(S,0,1)
         X(1,0); X(1,1)
-        EP(0,2); EP(0,3)
-        PR(1,2); PR(1,3)
-        EX(S,1,0); EX(V,1,1)
-        X(0,2); X(0,3)
-        EP(1,2); EPV(1,3)
-        QT(0,2); QT(1,2)
-        EX(S,0,2); EX(S,0,3)
-        X(1,2)
-        EX(V,1,2)
+        EP(0,2); EP(1,2)
+        X(0,2)
+        EX(V,1,0); EX(S,1,1)
+        QT(1,2,1); QT(0,2,1)
+        PR(0,3); PR(1,3)
+        EX(S,0,2)
+        EP(0,3); EP(1,3)
+        X(1,2); X(0,3)
+        QT(0,3,1); QT(1,3,1)
+        EX(S,1,2)
+        EX(V,0,3)
         XL(1,3)

@@ -262,12 +262,12 @@ def tile_stc_cell_pa_kernel(tc, Gs, Xt, Ht_1, out_0, out_1):
             nc.sync.dma_start(out=out.rearrange("b (m p) c l -> p (b m) (c l)", p=P)[:, m, :], in_=result[:, m, :])
 
         W(4)
-        T(0); W(1)
+        T(0); W(2)
         T(1); W(2)
         E(S,0,0); E(S,0,1); E(S,1,0); E(S,1,1)
         IG(V,0,4)
         QLH(0,0); QG(0,4); QLH(0,1)
-        T(2); W(1)
+        T(2); W(2)
         T(3)
         QLH(1,0); QLH(1,1)
         IG(S,0,6)

from contextlib import ExitStack

import concourse.mybir as mybir
from concourse.masks import make_identity

BF16 = mybir.dt.bfloat16
F32 = mybir.dt.float32
U32 = mybir.dt.uint32
U8 = mybir.dt.uint8
FP8X4 = mybir.dt.float8_e4m3fn_x4
COPY = mybir.ActivationFunctionType.Copy
MULT = mybir.AluOpType.mult
SUBTRACT = mybir.AluOpType.subtract

P = 128
PACK = 4
K_PASS = P * PACK
NODES = 1024
PASSES = NODES // K_PASS
TILES = NODES // P
PAIRS = TILES // 2
CHANNELS = 4
HALF_FEATS = 64
SOURCE_FEATS = CHANNELS * HALF_FEATS
FEATS = 2 * SOURCE_FEATS

FLOPS = 2 * NODES * NODES * NODES + 2 * 2 * NODES * NODES * FEATS


def tile_stc_cell_pa_kernel(tc, Gs, Xt, Ht_1, out_0, out_1):
    nc = tc.nc
    with ExitStack() as stack:
        keep = stack.enter_context(tc.tile_pool(name="keep", bufs=1))
        psum = stack.enter_context(tc.psum_pool(name="psum", bufs=8))
        stack.enter_context(tc.manual_schedule())

        g_rows = keep.tile([P, PASSES * PACK, NODES], BF16)
        g_dram = Gs.rearrange("(c p e) m -> c p e m", p=P, e=2)
        for c in range(4):
            nc.sync.dma_start(out=g_rows[:, 2 * c : 2 * c + 2, :], in_=g_dram[c])
        x_rows = keep.tile([P, 2, PASSES, PACK, SOURCE_FEATS], BF16)
        for s, source in enumerate((Xt, Ht_1)):
            nc.sync.dma_start(
                out=x_rows[:, s, :, :, :].rearrange("p g (u e) f -> p (g u) (e f)", e=2),
                in_=source.rearrange("b (k p e) c l -> p (b k) (e c l)", p=P, e=2),
            )

        zeros = keep.tile([P, K_PASS], BF16)
        nc.vector.memset(zeros[:].bitcast(U32), 0)
        ident = keep.tile([P, P], F32)
        make_identity(nc, ident[:])
        eye = keep.tile([P, K_PASS, PACK], BF16)
        nc.vector.memset(eye[:], 0.0)
        for u in range(2):
            nc.vector.tensor_copy(
                out=eye[:].rearrange("p (u q e) t -> p u q (e t)", u=2, e=2)[:, u, :, 2 * u : 2 * u + PACK + 2 : PACK + 1],
                in_=ident[:].unsqueeze(2).to_broadcast([P, P, 2]),
            )

        left_grouped = keep.tile([P, PAIRS, PASSES, 2 * P * PACK], BF16, align_bytes=64)
        left_codes = keep.tile([P, PAIRS, PASSES, 2 * P], U32, align_bytes=64)
        left_scales = keep.tile([P, PAIRS, PASSES, 2 * P], U8, align_bytes=64)
        g_grouped = keep.tile([P, PAIRS, PASSES, 2 * P, PACK], BF16, align_bytes=64)
        g_codes = keep.tile([P, PAIRS, PASSES, 2 * P], U32, align_bytes=64)
        g_scales = keep.tile([P, PAIRS, PASSES, 2 * P], U8, align_bytes=64)
        t2_grouped = keep.tile([P, PAIRS, PASSES, 2 * P, PACK], BF16, align_bytes=64)
        t2_codes = keep.tile([P, PAIRS, PASSES, 2 * P], U32, align_bytes=64)
        t2_scales = keep.tile([P, PAIRS, PASSES, 2 * P], U8, align_bytes=64)
        x_grouped = keep.tile([P, PASSES, FEATS, PACK], BF16, align_bytes=64)
        x_codes = keep.tile([P, PASSES, FEATS], U32, align_bytes=64)
        x_scales = keep.tile([P, PASSES, FEATS], U8, align_bytes=64)
        x1_sb = keep.tile([P, TILES, FEATS], F32)
        x2_sb = keep.tile([P, TILES, FEATS], F32)

        V = nc.vector.tensor_copy
        S = nc.scalar.copy
        banks = {}

        def quantise(grouped, codes, scales):
            nc.vector.quantize_mx(out=codes.bitcast(FP8X4), scales=scales, in_=grouped)

        def both_passes(grouped, codes, scales, j):
            flat = grouped[:, j, :, :] if len(grouped.shape) == 4 else grouped[:, j, :, :, :].rearrange("p h m t -> p h (m t)")
            quantise(
                flat.rearrange("p h n -> p (h n)"),
                codes[:, j, :, :].rearrange("p h n -> p (h n)"),
                scales[:, j, :, :].rearrange("p h n -> p (h n)"),
            )

        def one_pass(grouped, codes, scales, h, w, n):
            cols = slice(P * (w % 2), P * (w % 2 + n))
            quantise(grouped[:, w // 2, h, cols, :].rearrange("p m t -> p (m t)"), codes[:, w // 2, h, cols], scales[:, w // 2, h, cols])

        def regroup(copy, grouped, rows):
            copy(
                out=grouped.rearrange("p (c i) t -> p c t i", i=8),
                in_=rows.rearrange("p t (c i) -> p c t i", i=8),
            )

        def W(n):
            idle = psum.tile([P, K_PASS], F32, tag="bank")
            for i in range(n):
                nc.tensor.matmul(out=idle[:], lhsT=zeros[:, 0:P], rhs=zeros[:], start=True, stop=True)

        def T1(i):
            flipped = psum.tile([P, 2, 2, P], F32, tag="bank")
            banks["T1", i] = flipped
            words = g_rows[:, i, :].bitcast(F32).rearrange("p (h u q) -> p h u q", h=PASSES, u=2)
            for h in range(PASSES):
                for u in range(2):
                    nc.tensor.transpose(flipped[:, h, u, :], words[:, h, u, :], ident[:])

        def E1(copy, i):
            first = (i % 2) * P * PACK
            copy(
                out=left_grouped[:, i // 2, :, first : first + P * PACK].bitcast(F32).rearrange("q h (p u) -> q h p u", u=2),
                in_=banks["T1", i][:].rearrange("q h u p -> q h p u"),
            )

        def T(c):
            for h in range(PASSES):
                flipped = psum.tile([P, 2, 2, P], F32, tag="bank")
                banks["T", c, h] = flipped
                for i in range(2):
                    words = g_rows[:, 2 * c + i, :].bitcast(F32).rearrange("p (h u q) -> p h u q", h=PASSES, u=2)
                    for u in range(2):
                        nc.tensor.transpose(flipped[:, i, u, :], words[:, h, u, :], ident[:])

        def E(copy, c, h):
            copy(
                out=left_grouped[:, c, h, :].bitcast(F32).rearrange("q (i p u) -> q i p u", i=2, u=2),
                in_=banks["T", c, h][:].rearrange("q i u p -> q i p u"),
            )

        def QL(c):
            both_passes(left_grouped, left_codes, left_scales, c)

        def QLH(c, h):
            quantise(left_grouped[:, c, h, :], left_codes[:, c, h, :], left_scales[:, c, h, :])

        def IG(copy, h, w, n=2):
            cols = slice(P * (w % 2), P * (w % 2 + n))
            regroup(copy, g_grouped[:, w // 2, h, cols, :], g_rows[:, PACK * h : PACK * (h + 1), P * w : P * (w + n)])

        def QG(h, w, n=2):
            one_pass(g_grouped, g_codes, g_scales, h, w, n)

        def QGG(w):
            both_passes(g_grouped, g_codes, g_scales, w // 2)

        def IX(copy, s, g):
            regroup(copy, x_grouped[:, g, SOURCE_FEATS * s : SOURCE_FEATS * (s + 1), :], x_rows[:, s, g, :, :])

        def QX(g):
            quantise(x_grouped[:, g, :, :].rearrange("p f t -> p (f t)"), x_codes[:, g, :], x_scales[:, g, :])

        def QXX():
            quantise(
                x_grouped[:].rearrange("p g f t -> p (g f t)"),
                x_codes[:].rearrange("p g f -> p (g f)"),
                x_scales[:].rearrange("p g f -> p (g f)"),
            )

        def PR(g, w):
            cols = slice(P * (w % 2), P * (w % 2 + 1))
            product = psum.tile([P, PACK, P], F32, tag="bank")
            banks["P", g, w] = product
            for t in range(PACK):
                j = 2 * g + t // 2
                rows = slice(P * (t % 2), P * (t % 2 + 1))
                for h in range(PASSES):
                    nc.tensor.matmul_mx(
                        out=product[:, t, :],
                        lhsT=left_codes[:, j, h, rows].bitcast(FP8X4),
                        lhsT_scale=left_scales[:, j, h, rows],
                        rhs=g_codes[:, w // 2, h, cols].bitcast(FP8X4),
                        rhs_scale=g_scales[:, w // 2, h, cols],
                        start=(h == 0),
                        stop=(h == PASSES - 1),
                    )

        def EP(g, w):
            cols = slice(P * (w % 2), P * (w % 2 + 1))
            product = banks["P", g, w]
            if w // PACK == g:
                nc.vector.scalar_tensor_tensor(
                    out=t2_grouped[:, w // 2, g, cols, :],
                    in0=product[:].rearrange("p t m -> p m t"),
                    scalar=2.0,
                    in1=eye[:, P * (w % PACK) : P * (w % PACK + 1), :],
                    op0=MULT,
                    op1=SUBTRACT,
                )
            else:
                nc.scalar.activation(
                    out=t2_grouped[:, w // 2, g, cols, :], in_=product[:].rearrange("p t m -> p m t"), func=COPY, scale=2.0
                )

        def EPV(g, w):
            cols = slice(P * (w % 2), P * (w % 2 + 1))
            nc.vector.tensor_scalar(
                out=t2_grouped[:, w // 2, g, cols, :],
                in0=banks["P", g, w][:].rearrange("p t m -> p m t"),
                scalar1=2.0,
                scalar2=None,
                op0=MULT,
            )

        def QT(g, w, n=2):
            one_pass(t2_grouped, t2_codes, t2_scales, g, w, n)

        def QTT(w):
            both_passes(t2_grouped, t2_codes, t2_scales, w // 2)

        def X(k, m):
            codes, scales = ((g_codes, g_scales), (t2_codes, t2_scales))[k]
            cols = slice(P * (m % 2), P * (m % 2 + 1))
            acc = psum.tile([P, FEATS], F32, tag="bank")
            banks["X", k, m] = acc
            for g in range(PASSES):
                nc.tensor.matmul_mx(
                    out=acc[:],
                    lhsT=codes[:, m // 2, g, cols].bitcast(FP8X4),
                    lhsT_scale=scales[:, m // 2, g, cols],
                    rhs=x_codes[:, g, :].bitcast(FP8X4),
                    rhs_scale=x_scales[:, g, :],
                    start=(g == 0),
                    stop=(g == PASSES - 1),
                )

        def EX(copy, k, m):
            result, out = ((x1_sb, out_0), (x2_sb, out_1))[k]
            copy(
                out=result[:, m, :].rearrange("p (c s l) -> p s c l", c=CHANNELS, s=2),
                in_=banks["X", k, m][:].rearrange("p (s c l) -> p s c l", s=2, c=CHANNELS),
            )
            nc.sync.dma_start(out=out.rearrange("b (m p) c l -> p (b m) (c l)", p=P)[:, m, :], in_=result[:, m, :])

        def XL(k, m):
            codes, scales = ((g_codes, g_scales), (t2_codes, t2_scales))[k]
            result, out = ((x1_sb, out_0), (x2_sb, out_1))[k]
            cols = slice(P * (m % 2), P * (m % 2 + 1))
            for pair, copy in enumerate((V, S)):
                acc = psum.tile([P, 2, P], F32, tag="bank")
                for s in range(2):
                    feats = slice(SOURCE_FEATS * s + P * pair, SOURCE_FEATS * s + P * (pair + 1))
                    for g in range(PASSES):
                        nc.tensor.matmul_mx(
                            out=acc[:, s, :],
                            lhsT=codes[:, m // 2, g, cols].bitcast(FP8X4),
                            lhsT_scale=scales[:, m // 2, g, cols],
                            rhs=x_codes[:, g, feats].bitcast(FP8X4),
                            rhs_scale=x_scales[:, g, feats],
                            start=(g == 0),
                            stop=(g == PASSES - 1),
                        )
                part = slice(2 * P * pair, 2 * P * (pair + 1))
                copy(
                    out=result[:, m, part].rearrange("p (c s l) -> p s c l", c=2, s=2),
                    in_=acc[:].rearrange("p s (c l) -> p s c l", c=2),
                )
            nc.sync.dma_start(out=out.rearrange("b (m p) c l -> p (b m) (c l)", p=P)[:, m, :], in_=result[:, m, :])

        W(4)
        T(0); W(2)
        T(1); W(2)
        E(S,0,0); E(S,0,1); E(S,1,0); E(S,1,1)
        IG(V,0,4)
        QLH(0,0); QG(0,4); QLH(0,1)
        T(2); W(2)
        T(3)
        QLH(1,0); QLH(1,1)
        IG(S,0,6)
        IG(V,1,4,1); IG(V,1,5,1); QG(1,4,1); QG(1,5,1)
        PR(0,4); PR(0,5)
        IG(V,1,6); QG(0,6); QG(1,6)
        E(S,2,0); E(S,2,1); E(S,3,0); E(S,3,1)
        PR(0,6); PR(0,7)
        QLH(2,0); QLH(2,1); QLH(3,0); QLH(3,1)
        IX(S,0,0); IX(S,0,1)
        PR(1,4); PR(1,5)
        IX(V,1,0); IX(V,1,1)
        QX(0); QX(1)
        EP(0,4); EP(0,5)
        PR(1,6); PR(1,7)
        EP(0,6); EP(0,7)
        EP(1,4)
        X(0,4); X(0,5)
        EP(1,5)
        QT(0,4); QT(1,4)
        EP(1,6); EP(1,7)
        IG(S,1,0); IG(S,0,0)
        X(0,6); X(0,7)
        QT(0,6); QT(1,6)
        X(1,4); X(1,5)
        EX(S,0,4); EX(S,0,5)
        QG(1,0); QG(0,0)
        X(1,6); X(1,7)
        EX(S,0,6); EX(S,0,7)
        IG(V,0,2); IG(V,1,2)
        PR(0,0); PR(0,1)
        EX(S,1,4); EX(V,1,5)
        QG(0,2); QG(1,2)
        PR(1,0); PR(1,1)
        EX(S,1,6); EX(V,1,7)
        EP(0,0); EP(0,1)
        X(0,0); X(0,1)
        EP(1,0); EP(1,1)
        QT(1,0); QT(0,0)
        PR(0,2); PR(1,2)
        EX(S,0,0); EX(S,0,1)
        X(1,0); X(1,1)
        EP(0,2); EP(1,2)
        X(0,2)
        EX(V,1,0); EX(S,1,1)
        QT(1,2,1); QT(0,2,1)
        PR(0,3); PR(1,3)
        EX(S,0,2)
        EP(0,3); EP(1,3)
        X(1,2); X(0,3)
        QT(0,3,1); QT(1,3,1)
        EX(S,1,2)
        EX(V,0,3)
        XL(1,3)
